import numpy as np
import ml_dtypes


def mxq(x, axis, fmt="e4m3"):
    dtype, down = {"e4m3": (ml_dtypes.float8_e4m3fn, 7), "e5m2": (ml_dtypes.float8_e5m2, 14)}[fmt]
    v = np.moveaxis(np.asarray(x, np.float32).astype(ml_dtypes.bfloat16).astype(np.float64), axis, -1)
    blocks = v.reshape(v.shape[:-1] + (-1, 32))
    amax = np.abs(blocks).max(-1, keepdims=True)
    byte = np.maximum(np.where(amax > 0, np.frexp(amax)[1] - 1 + 127, 0) - down, 1)
    scale = np.exp2(byte - 127.0)
    codes = (blocks / scale).astype(np.float32).astype(dtype).astype(np.float64)
    return np.moveaxis((codes * scale).reshape(v.shape), -1, axis)


WIDE = False


def mx_kscale(k):
    if not WIDE:
        return np.ones(k)
    levels = np.array([10, -10, 5, -5, 0])
    a = np.random.permutation(np.resize(levels, k // 512 * 4)).reshape(k // 512, 4)
    idx = np.arange(k)
    return np.exp2(a[idx // 512, idx % 128 // 32])


BF16 = ml_dtypes.bfloat16


def bf(x):
    return np.asarray(x, np.float32).astype(BF16)


def f64(x):
    return np.asarray(x).astype(np.float64)


B, C, HH, WW = 1, 1024, 8, 16
N = HH * WW


def setup_inputs():
    s, t = mx_kscale(C), mx_kscale(C)
    return {"x": bf(np.random.standard_normal((B, C, HH, WW)) * s[None, :, None, None]),
            "Wq": bf(np.random.standard_normal((C, C)) * 1.4 / np.sqrt(C) * t[:, None] / s[None, :]),
            "bq": bf(np.random.standard_normal(C) * 0.2 * t),
            "k": bf(np.random.standard_normal((B, N, C)) * 1.4 / t)}


def reference(x, Wq, bq, k):
    xt = f64(x).reshape(B, C, N)
    q = (mxq(xt, 1, "e4m3").transpose(0, 2, 1) @ mxq(f64(Wq), 1, "e4m3").T) + f64(bq)
    scores = mxq(q / np.sqrt(C), 2, "e4m3") @ mxq(f64(k), 2, "e4m3").transpose(0, 2, 1)
    e = np.exp(scores - scores.max(-1, keepdims=True))
    return e / e.sum(-1, keepdims=True)

@@ -1,0 +1,220 @@
+from contextlib import ExitStack
+
+import concourse.mybir as mybir
+from concourse.masks import make_identity
+
+F32 = mybir.dt.float32
+BF16 = mybir.dt.bfloat16
+U32 = mybir.dt.uint32
+U8 = mybir.dt.uint8
+FP8X4 = mybir.dt.float8_e4m3fn_x4
+ACT = mybir.ActivationFunctionType
+ALU = mybir.AluOpType
+AXIS = mybir.AxisListType
+
+P = 128
+TOKENS = 128
+CHANNELS = 1024
+PACK = 4
+K_PASS = P * PACK
+PASSES = CHANNELS // K_PASS
+PAIR = 2
+HALVES = PACK // PAIR
+O_TILES = CHANNELS // P
+GROUPS = PASSES * HALVES
+TILES_PER_LOAD = PAIR
+TILES_PER_PASS = O_TILES // PASSES
+VECTOR_EVERY = 4
+
+FLOPS = 2 * TOKENS * CHANNELS * CHANNELS + 2 * TOKENS * TOKENS * CHANNELS
+
+
+def tile_visionattention_pa_s_kernel(tc, x, Wq, bq, k, out):
+    nc = tc.nc
+    with ExitStack() as ctx:
+        ctx.enter_context(tc.manual_schedule())
+        keep = ctx.enter_context(tc.tile_pool(name="keep", bufs=1))
+        per_tile = ctx.enter_context(tc.tile_pool(name="per_tile", bufs=O_TILES))
+        per_pass = ctx.enter_context(tc.tile_pool(name="per_pass", bufs=PASSES))
+        psum_w = ctx.enter_context(tc.psum_pool(name="psum_w", bufs=4))
+        psum_q = ctx.enter_context(tc.psum_pool(name="psum_q", bufs=PASSES))
+        psum_one = ctx.enter_context(tc.psum_pool(name="psum_one", bufs=1))
+
+        bq_rows = keep.tile([P, PAIR * P], BF16)
+        nc.vector.memset(bq_rows[:], 0.0)
+        zero_col = keep.tile([P, 1], F32)
+        nc.vector.memset(zero_col[:], 0.0)
+        nc.scalar.dma_start(
+            out=bq_rows[0:GROUPS, :], in_=bq.rearrange("(a w) -> a w", a=GROUPS)
+        )
+
+        k_sb = keep.tile([P, CHANNELS], BF16)
+        nc.sync.dma_start(out=k_sb[:], in_=k.rearrange("b m c -> (b m) c"))
+
+        x_sb = keep.tile([P, CHANNELS], BF16)
+        nc.sync.dma_start(
+            out=x_sb[:].rearrange("p (a en) -> p a en", a=GROUPS),
+            in_=x.rearrange("b c h w -> c (b h w)").rearrange(
+                "(a p e) n -> p a (e n)", p=P, e=PAIR
+            ),
+        )
+
+        wq_sb = keep.tile([P, O_TILES * CHANNELS], BF16)
+        wq_loads = wq_sb[:].rearrange("p (a ec) -> p a ec", a=GROUPS)
+        wq_rows = Wq.rearrange("(a r e) c -> r a (e c)", r=P, e=PAIR)
+        for a in range(GROUPS):
+            nc.sync.dma_start(out=wq_loads[:, a, :], in_=wq_rows[:, a, :])
+        wq_words = wq_sb[:].bitcast(F32).rearrange("p (j w) -> p j w", j=O_TILES)
+
+        ident = keep.tile([P, P], F32)
+        make_identity(nc, ident[:])
+
+        warm = keep.tile([P, 1], F32)
+        nc.scalar.activation(out=warm[:], in_=zero_col[:], func=ACT.Exp)
+
+        k_words = k_sb[:].bitcast(F32)
+        kT = psum_one.tile([P, PASSES, HALVES, TOKENS], F32)
+        for g in range(PASSES):
+            for u in range(HALVES):
+                first = (g * HALVES + u) * P
+                nc.tensor.transpose(kT[:, g, u, :], k_words[:, first : first + P], ident[:])
+        k_grouped = keep.tile([P, PASSES * TOKENS * PACK], BF16, align_bytes=64)
+        nc.scalar.copy(
+            out=k_grouped[:].bitcast(F32).rearrange("p (g m u) -> p g m u", g=PASSES, u=HALVES),
+            in_=kT[:].rearrange("p g u m -> p g m u"),
+        )
+
+        bqT = psum_one.tile([P, P], F32, tag="small")
+        nc.tensor.transpose(bqT[:], bq_rows[:].bitcast(F32), ident[:])
+
+        x_grouped = keep.tile([P, PASSES * TOKENS * PACK], BF16, align_bytes=64)
+        nc.vector.tensor_copy(
+            out=x_grouped[:].rearrange("p (g n t) -> p g n t", g=PASSES, t=PACK),
+            in_=x_sb[:].rearrange("p (g t n) -> p g n t", g=PASSES, t=PACK),
+        )
+        bias = keep.tile([P, O_TILES], F32)
+        nc.vector.tensor_scalar(
+            out=bias[:],
+            in0=bqT[:, 0:GROUPS].bitcast(BF16),
+            scalar1=1.0 / 32.0,
+            scalar2=None,
+            op0=ALU.mult,
+        )
+        k_codes = keep.tile([P, PASSES * TOKENS], U32, align_bytes=64)
+        k_scales = keep.tile([P, PASSES * TOKENS], U8, align_bytes=64)
+        nc.vector.quantize_mx(out=k_codes[:].bitcast(FP8X4), scales=k_scales[:], in_=k_grouped[:])
+        x_codes = keep.tile([P, PASSES * TOKENS], U32, align_bytes=64)
+        x_scales = keep.tile([P, PASSES * TOKENS], U8, align_bytes=64)
+        nc.vector.quantize_mx(out=x_codes[:].bitcast(FP8X4), scales=x_scales[:], in_=x_grouped[:])
+
+        w_banks = []
+        w_grouped = []
+        w_codes = []
+        w_scales = []
+        qT = []
+        q_codes = []
+        q_scales = []
+
+        def transpose_wq_tile(j):
+            wT = psum_w.tile([P, PASSES, HALVES, P], F32)
+            for g in range(PASSES):
+                for u in range(HALVES):
+                    first = (g * HALVES + u) * P
+                    nc.tensor.transpose(wT[:, g, u, :], wq_words[:, j, first : first + P], ident[:])
+            w_banks.append(wT)
+
+        def empty_wq_bank(j):
+            grouped = per_tile.tile([P, PASSES * P * PACK], BF16, align_bytes=64)
+            copy = nc.vector.tensor_copy if j % VECTOR_EVERY == VECTOR_EVERY - 1 else nc.scalar.copy
+            copy(
+                out=grouped[:].bitcast(F32).rearrange("p (g r u) -> p g r u", g=PASSES, u=HALVES),
+                in_=w_banks[j][:].rearrange("p g u r -> p g r u"),
+            )
+            w_grouped.append(grouped)
+
+        def quantise_wq_tile(j):
+            codes = per_tile.tile([P, PASSES * P], U32, align_bytes=64)
+            scales = per_tile.tile([P, PASSES * P], U8, align_bytes=64)
+            nc.vector.quantize_mx(out=codes[:].bitcast(FP8X4), scales=scales[:], in_=w_grouped[j][:])
+            w_codes.append(codes)
+            w_scales.append(scales)
+
+        def project_tile(j):
+            if j % TILES_PER_PASS == 0:
+                q_bank = psum_q.tile([P, TILES_PER_PASS, TOKENS], F32)
+                qT.append(q_bank)
+            for g in range(PASSES):
+                cols = slice(g * P, (g + 1) * P)
+                nc.tensor.matmul_mx(
+                    out=qT[j // TILES_PER_PASS][:, j % TILES_PER_PASS, :],
+                    lhsT=w_codes[j][:, cols].bitcast(FP8X4),
+                    lhsT_scale=w_scales[j][:, cols],
+                    rhs=x_codes[:, cols].bitcast(FP8X4),
+                    rhs_scale=x_scales[:, cols],
+                    start=(g == 0),
+                    stop=(g == PASSES - 1),
+                )
+
+        def finish_q_pass(g):
+            grouped = per_pass.tile([P, TOKENS * PACK], BF16, align_bytes=64)
+            nc.vector.scalar_tensor_tensor(
+                out=grouped[:].rearrange("p (n t) -> p n t", t=PACK),
+                in0=qT[g][:].rearrange("p t n -> p n t"),
+                scalar=1.0 / 32.0,
+                in1=bias[:, g * PACK : (g + 1) * PACK].unsqueeze(1).to_broadcast([P, TOKENS, PACK]),
+                op0=ALU.mult,
+                op1=ALU.add,
+            )
+            codes = per_pass.tile([P, TOKENS], U32, align_bytes=64)
+            scales = per_pass.tile([P, TOKENS], U8, align_bytes=64)
+            nc.vector.quantize_mx(out=codes[:].bitcast(FP8X4), scales=scales[:], in_=grouped[:])
+            q_codes.append(codes)
+            q_scales.append(scales)
+
+        scores = psum_one.tile([P, TOKENS], F32, tag="small")
+
+        def score_pass(g):
+            cols = slice(g * TOKENS, (g + 1) * TOKENS)
+            nc.tensor.matmul_mx(
+                out=scores[:],
+                lhsT=q_codes[g][:].bitcast(FP8X4),
+                lhsT_scale=q_scales[g][:],
+                rhs=k_codes[:, cols].bitcast(FP8X4),
+                rhs_scale=k_scales[:, cols],
+                start=(g == 0),
+                stop=(g == PASSES - 1),
+            )
+
+        def tiles_of_load(a):
+            if 0 <= a < GROUPS:
+                return range(a * TILES_PER_LOAD, (a + 1) * TILES_PER_LOAD)
+            return range(0)
+
+        for a in range(GROUPS + 1):
+            for j in tiles_of_load(a):
+                transpose_wq_tile(j)
+            for j in tiles_of_load(a - 1):
+                quantise_wq_tile(j)
+            for j in tiles_of_load(a):
+                empty_wq_bank(j)
+            for j in tiles_of_load(a - 1):
+                project_tile(j)
+            if a > 0 and a % HALVES == 0:
+                finish_q_pass(a // HALVES - 1)
+        for g in range(PASSES):
+            score_pass(g)
+
+        neg_max = keep.tile([P, 1], F32)
+        nc.vector.tensor_reduce(out=neg_max[:], in_=scores[:], axis=AXIS.X, op=ALU.max, negate=True)
+        expo = keep.tile([P, TOKENS], F32)
+        row_sum = keep.tile([P, 1], F32)
+        nc.scalar.activation(
+            out=expo[:], in_=scores[:], func=ACT.Exp, bias=neg_max[:], scale=1.0, accum_out=row_sum[:]
+        )
+        inv_sum = keep.tile([P, 1], F32)
+        nc.vector.reciprocal(out=inv_sum[:], in_=row_sum[:])
+        prob = keep.tile([P, TOKENS], F32)
+        nc.vector.tensor_scalar(
+            out=prob[:], in0=expo[:], scalar1=inv_sum[:, 0:1], scalar2=None, op0=ALU.mult
+        )
+        nc.sync.dma_start(out=out.rearrange("b n m -> (b n) m"), in_=prob[:])

@@ -20,11 +20,12 @@ K_PASS = P * PACK
 PASSES = CHANNELS // K_PASS
 PAIR = 2
 HALVES = PACK // PAIR
-O_TILES = CHANNELS // P
 GROUPS = PASSES * HALVES
-TILES_PER_LOAD = PAIR
+O_TILES = CHANNELS // P
 TILES_PER_PASS = O_TILES // PASSES
-VECTOR_EVERY = 4
+ROUND_TILES = 2
+ROUNDS = O_TILES // ROUND_TILES
+ROUNDS_PER_PASS = TILES_PER_PASS // ROUND_TILES
 
 FLOPS = 2 * TOKENS * CHANNELS * CHANNELS + 2 * TOKENS * TOKENS * CHANNELS
 
@@ -36,7 +37,7 @@ def tile_visionattention_pa_s_kernel(tc, x, Wq, bq, k, out):
         keep = ctx.enter_context(tc.tile_pool(name="keep", bufs=1))
         per_tile = ctx.enter_context(tc.tile_pool(name="per_tile", bufs=O_TILES))
         per_pass = ctx.enter_context(tc.tile_pool(name="per_pass", bufs=PASSES))
-        psum_w = ctx.enter_context(tc.psum_pool(name="psum_w", bufs=4))
+        psum_t = ctx.enter_context(tc.psum_pool(name="psum_t", bufs=4))
         psum_q = ctx.enter_context(tc.psum_pool(name="psum_q", bufs=PASSES))
         psum_one = ctx.enter_context(tc.psum_pool(name="psum_one", bufs=1))
 
@@ -48,23 +49,23 @@ def tile_visionattention_pa_s_kernel(tc, x, Wq, bq, k, out):
             out=bq_rows[0:GROUPS, :], in_=bq.rearrange("(a w) -> a w", a=GROUPS)
         )
 
-        k_sb = keep.tile([P, CHANNELS], BF16)
-        nc.sync.dma_start(out=k_sb[:], in_=k.rearrange("b m c -> (b m) c"))
-
+        wq_sb = keep.tile([P, O_TILES * CHANNELS], BF16)
+        wq_tiles = wq_sb[:].rearrange("p (j c) -> p j c", j=O_TILES)
+        wq_rows = Wq.rearrange("(a r e) c -> r a e c", r=P, e=PAIR)
         x_sb = keep.tile([P, CHANNELS], BF16)
+        k_sb = keep.tile([P, CHANNELS], BF16)
+        nc.sync.dma_start(out=wq_tiles[:, 0, :], in_=wq_rows[:, 0, 0, :])
         nc.sync.dma_start(
             out=x_sb[:].rearrange("p (a en) -> p a en", a=GROUPS),
             in_=x.rearrange("b c h w -> c (b h w)").rearrange(
                 "(a p e) n -> p a (e n)", p=P, e=PAIR
             ),
         )
-
-        wq_sb = keep.tile([P, O_TILES * CHANNELS], BF16)
-        wq_loads = wq_sb[:].rearrange("p (a ec) -> p a ec", a=GROUPS)
-        wq_rows = Wq.rearrange("(a r e) c -> r a (e c)", r=P, e=PAIR)
-        for a in range(GROUPS):
-            nc.sync.dma_start(out=wq_loads[:, a, :], in_=wq_rows[:, a, :])
+        for j in range(1, O_TILES):
+            nc.sync.dma_start(out=wq_tiles[:, j, :], in_=wq_rows[:, j // PAIR, j % PAIR, :])
+        nc.sync.dma_start(out=k_sb[:], in_=k.rearrange("b m c -> (b m) c"))
         wq_words = wq_sb[:].bitcast(F32).rearrange("p (j w) -> p j w", j=O_TILES)
+        k_words = k_sb[:].bitcast(F32)
 
         ident = keep.tile([P, P], F32)
         make_identity(nc, ident[:])
@@ -72,88 +73,56 @@ def tile_visionattention_pa_s_kernel(tc, x, Wq, bq, k, out):
         warm = keep.tile([P, 1], F32)
         nc.scalar.activation(out=warm[:], in_=zero_col[:], func=ACT.Exp)
 
-        k_words = k_sb[:].bitcast(F32)
-        kT = psum_one.tile([P, PASSES, HALVES, TOKENS], F32)
-        for g in range(PASSES):
-            for u in range(HALVES):
-                first = (g * HALVES + u) * P
-                nc.tensor.transpose(kT[:, g, u, :], k_words[:, first : first + P], ident[:])
-        k_grouped = keep.tile([P, PASSES * TOKENS * PACK], BF16, align_bytes=64)
-        nc.scalar.copy(
-            out=k_grouped[:].bitcast(F32).rearrange("p (g m u) -> p g m u", g=PASSES, u=HALVES),
-            in_=kT[:].rearrange("p g u m -> p g m u"),
-        )
-
-        bqT = psum_one.tile([P, P], F32, tag="small")
-        nc.tensor.transpose(bqT[:], bq_rows[:].bitcast(F32), ident[:])
-
         x_grouped = keep.tile([P, PASSES * TOKENS * PACK], BF16, align_bytes=64)
         nc.vector.tensor_copy(
             out=x_grouped[:].rearrange("p (g n t) -> p g n t", g=PASSES, t=PACK),
             in_=x_sb[:].rearrange("p (g t n) -> p g n t", g=PASSES, t=PACK),
         )
-        bias = keep.tile([P, O_TILES], F32)
-        nc.vector.tensor_scalar(
-            out=bias[:],
-            in0=bqT[:, 0:GROUPS].bitcast(BF16),
-            scalar1=1.0 / 32.0,
-            scalar2=None,
-            op0=ALU.mult,
-        )
-        k_codes = keep.tile([P, PASSES * TOKENS], U32, align_bytes=64)
-        k_scales = keep.tile([P, PASSES * TOKENS], U8, align_bytes=64)
-        nc.vector.quantize_mx(out=k_codes[:].bitcast(FP8X4), scales=k_scales[:], in_=k_grouped[:])
         x_codes = keep.tile([P, PASSES * TOKENS], U32, align_bytes=64)
         x_scales = keep.tile([P, PASSES * TOKENS], U8, align_bytes=64)
         nc.vector.quantize_mx(out=x_codes[:].bitcast(FP8X4), scales=x_scales[:], in_=x_grouped[:])
 
-        w_banks = []
-        w_grouped = []
-        w_codes = []
-        w_scales = []
-        qT = []
-        q_codes = []
-        q_scales = []
-
-        def transpose_wq_tile(j):
-            wT = psum_w.tile([P, PASSES, HALVES, P], F32)
+        def transpose_rows(words):
+            bank = psum_t.tile([P, PASSES, HALVES, P], F32)
             for g in range(PASSES):
                 for u in range(HALVES):
                     first = (g * HALVES + u) * P
-                    nc.tensor.transpose(wT[:, g, u, :], wq_words[:, j, first : first + P], ident[:])
-            w_banks.append(wT)
+                    nc.tensor.transpose(bank[:, g, u, :], words[:, first : first + P], ident[:])
+            return bank
 
-        def empty_wq_bank(j):
-            grouped = per_tile.tile([P, PASSES * P * PACK], BF16, align_bytes=64)
-            copy = nc.vector.tensor_copy if j % VECTOR_EVERY == VECTOR_EVERY - 1 else nc.scalar.copy
-            copy(
+        def empty_bank(bank):
+            grouped = per_tile.tile([P, PASSES * P * PACK], BF16, align_bytes=64, bufs=O_TILES + 1)
+            nc.scalar.copy(
                 out=grouped[:].bitcast(F32).rearrange("p (g r u) -> p g r u", g=PASSES, u=HALVES),
-                in_=w_banks[j][:].rearrange("p g u r -> p g r u"),
+                in_=bank[:].rearrange("p g u r -> p g r u"),
             )
-            w_grouped.append(grouped)
+            return grouped
 
-        def quantise_wq_tile(j):
-            codes = per_tile.tile([P, PASSES * P], U32, align_bytes=64)
-            scales = per_tile.tile([P, PASSES * P], U8, align_bytes=64)
-            nc.vector.quantize_mx(out=codes[:].bitcast(FP8X4), scales=scales[:], in_=w_grouped[j][:])
-            w_codes.append(codes)
-            w_scales.append(scales)
+        def quantise_rows(grouped):
+            codes = per_tile.tile([P, PASSES * P], U32, align_bytes=64, bufs=O_TILES + 1)
+            scales = per_tile.tile([P, PASSES * P], U8, align_bytes=64, bufs=O_TILES + 1)
+            nc.vector.quantize_mx(out=codes[:].bitcast(FP8X4), scales=scales[:], in_=grouped[:])
+            return codes, scales
 
-        def project_tile(j):
-            if j % TILES_PER_PASS == 0:
-                q_bank = psum_q.tile([P, TILES_PER_PASS, TOKENS], F32)
-                qT.append(q_bank)
+        qT = []
+        for g in range(PASSES):
+            q_bank = psum_q.tile([P, TILES_PER_PASS, TOKENS], F32)
+            qT.append(q_bank)
+
+        def project_tile(j, codes, scales):
             for g in range(PASSES):
                 cols = slice(g * P, (g + 1) * P)
                 nc.tensor.matmul_mx(
                     out=qT[j // TILES_PER_PASS][:, j % TILES_PER_PASS, :],
-                    lhsT=w_codes[j][:, cols].bitcast(FP8X4),
-                    lhsT_scale=w_scales[j][:, cols],
+                    lhsT=codes[:, cols].bitcast(FP8X4),
+                    lhsT_scale=scales[:, cols],
                     rhs=x_codes[:, cols].bitcast(FP8X4),
                     rhs_scale=x_scales[:, cols],
                     start=(g == 0),
                     stop=(g == PASSES - 1),
                 )
+
+        bias = keep.tile([P, O_TILES], F32)
 
         def finish_q_pass(g):
             grouped = per_pass.tile([P, TOKENS * PACK], BF16, align_bytes=64)
@@ -168,41 +137,58 @@ def tile_visionattention_pa_s_kernel(tc, x, Wq, bq, k, out):
             codes = per_pass.tile([P, TOKENS], U32, align_bytes=64)
             scales = per_pass.tile([P, TOKENS], U8, align_bytes=64)
             nc.vector.quantize_mx(out=codes[:].bitcast(FP8X4), scales=scales[:], in_=grouped[:])
-            q_codes.append(codes)
-            q_scales.append(scales)
+            return codes, scales
+
+        def tiles_of_round(a):
+            if 0 <= a < ROUNDS:
+                return range(a * ROUND_TILES, (a + 1) * ROUND_TILES)
+            return range(0)
+
+        banks = {}
+        grouped_rows = {}
+        quantised = {}
+        q_quantised = {}
+        for a in range(ROUNDS + 2):
+            for j in tiles_of_round(a):
+                banks[j] = transpose_rows(wq_words[:, j, :])
+            if a == 0:
+                bqT = psum_one.tile([P, P], F32, tag="small")
+                nc.tensor.transpose(bqT[:], bq_rows[:].bitcast(F32), ident[:])
+                nc.vector.tensor_scalar(
+                    out=bias[:],
+                    in0=bqT[:, 0:GROUPS].bitcast(BF16),
+                    scalar1=1.0 / 32.0,
+                    scalar2=None,
+                    op0=ALU.mult,
+                )
+            if a == ROUNDS:
+                banks["k"] = transpose_rows(k_words)
+            for j in tiles_of_round(a - 1):
+                quantised[j] = quantise_rows(grouped_rows[j])
+            if a == ROUNDS + 1:
+                quantised["k"] = quantise_rows(grouped_rows["k"])
+            if a >= 2 and (a - 1) % ROUNDS_PER_PASS == 0:
+                g = (a - 1) // ROUNDS_PER_PASS - 1
+                q_quantised[g] = finish_q_pass(g)
+            for j in tiles_of_round(a):
+                grouped_rows[j] = empty_bank(banks[j])
+            if a == ROUNDS:
+                grouped_rows["k"] = empty_bank(banks["k"])
+            for j in tiles_of_round(a - 1):
+                project_tile(j, quantised[j][0], quantised[j][1])
 
         scores = psum_one.tile([P, TOKENS], F32, tag="small")
-
-        def score_pass(g):
+        for g in range(PASSES):
             cols = slice(g * TOKENS, (g + 1) * TOKENS)
             nc.tensor.matmul_mx(
                 out=scores[:],
-                lhsT=q_codes[g][:].bitcast(FP8X4),
-                lhsT_scale=q_scales[g][:],
-                rhs=k_codes[:, cols].bitcast(FP8X4),
-                rhs_scale=k_scales[:, cols],
+                lhsT=q_quantised[g][0][:].bitcast(FP8X4),
+                lhsT_scale=q_quantised[g][1][:],
+                rhs=quantised["k"][0][:, cols].bitcast(FP8X4),
+                rhs_scale=quantised["k"][1][:, cols],
                 start=(g == 0),
                 stop=(g == PASSES - 1),
             )
-
-        def tiles_of_load(a):
-            if 0 <= a < GROUPS:
-                return range(a * TILES_PER_LOAD, (a + 1) * TILES_PER_LOAD)
-            return range(0)
-
-        for a in range(GROUPS + 1):
-            for j in tiles_of_load(a):
-                transpose_wq_tile(j)
-            for j in tiles_of_load(a - 1):
-                quantise_wq_tile(j)
-            for j in tiles_of_load(a):
-                empty_wq_bank(j)
-            for j in tiles_of_load(a - 1):
-                project_tile(j)
-            if a > 0 and a % HALVES == 0:
-                finish_q_pass(a // HALVES - 1)
-        for g in range(PASSES):
-            score_pass(g)
 
         neg_max = keep.tile([P, 1], F32)
         nc.vector.tensor_reduce(out=neg_max[:], in_=scores[:], axis=AXIS.X, op=ALU.max, negate=True)

@@ -26,6 +26,7 @@ TILES_PER_PASS = O_TILES // PASSES
 ROUND_TILES = 2
 ROUNDS = O_TILES // ROUND_TILES
 ROUNDS_PER_PASS = TILES_PER_PASS // ROUND_TILES
+WARM_BANKS = 4
 
 FLOPS = 2 * TOKENS * CHANNELS * CHANNELS + 2 * TOKENS * TOKENS * CHANNELS
 
@@ -40,6 +41,25 @@ def tile_visionattention_pa_s_kernel(tc, x, Wq, bq, k, out):
         psum_t = ctx.enter_context(tc.psum_pool(name="psum_t", bufs=4))
         psum_q = ctx.enter_context(tc.psum_pool(name="psum_q", bufs=PASSES))
         psum_one = ctx.enter_context(tc.psum_pool(name="psum_one", bufs=1))
+
+        zeros = keep.tile([P, P * PACK], BF16, align_bytes=64)
+        nc.vector.memset(zeros[:], 0.0)
+        zero_codes = keep.tile([P, P], U32, align_bytes=64)
+        zero_scales = keep.tile([P, P], U8, align_bytes=64)
+        nc.vector.quantize_mx(out=zero_codes[:].bitcast(FP8X4), scales=zero_scales[:], in_=zeros[:])
+        for b in range(WARM_BANKS):
+            bank = psum_t.tile([P, PASSES, HALVES, P], F32)
+            for g in range(PASSES):
+                for u in range(HALVES):
+                    nc.tensor.matmul_mx(
+                        out=bank[:, g, u, :],
+                        lhsT=zero_codes[:].bitcast(FP8X4),
+                        lhsT_scale=zero_scales[:],
+                        rhs=zero_codes[:].bitcast(FP8X4),
+                        rhs_scale=zero_scales[:],
+                        start=True,
+                        stop=True,
+                    )
 
         bq_rows = keep.tile([P, PAIR * P], BF16)
         nc.vector.memset(bq_rows[:], 0.0)

@@ -23,10 +23,9 @@ HALVES = PACK // PAIR
 GROUPS = PASSES * HALVES
 O_TILES = CHANNELS // P
 TILES_PER_PASS = O_TILES // PASSES
-ROUND_TILES = 2
+ROUND_TILES = 4
 ROUNDS = O_TILES // ROUND_TILES
 ROUNDS_PER_PASS = TILES_PER_PASS // ROUND_TILES
-WARM_BANKS = 4
 
 FLOPS = 2 * TOKENS * CHANNELS * CHANNELS + 2 * TOKENS * TOKENS * CHANNELS
 
@@ -42,25 +41,6 @@ def tile_visionattention_pa_s_kernel(tc, x, Wq, bq, k, out):
         psum_q = ctx.enter_context(tc.psum_pool(name="psum_q", bufs=PASSES))
         psum_one = ctx.enter_context(tc.psum_pool(name="psum_one", bufs=1))
 
-        zeros = keep.tile([P, P * PACK], BF16, align_bytes=64)
-        nc.vector.memset(zeros[:], 0.0)
-        zero_codes = keep.tile([P, P], U32, align_bytes=64)
-        zero_scales = keep.tile([P, P], U8, align_bytes=64)
-        nc.vector.quantize_mx(out=zero_codes[:].bitcast(FP8X4), scales=zero_scales[:], in_=zeros[:])
-        for b in range(WARM_BANKS):
-            bank = psum_t.tile([P, PASSES, HALVES, P], F32)
-            for g in range(PASSES):
-                for u in range(HALVES):
-                    nc.tensor.matmul_mx(
-                        out=bank[:, g, u, :],
-                        lhsT=zero_codes[:].bitcast(FP8X4),
-                        lhsT_scale=zero_scales[:],
-                        rhs=zero_codes[:].bitcast(FP8X4),
-                        rhs_scale=zero_scales[:],
-                        start=True,
-                        stop=True,
-                    )
-
         bq_rows = keep.tile([P, PAIR * P], BF16)
         nc.vector.memset(bq_rows[:], 0.0)
         zero_col = keep.tile([P, 1], F32)
@@ -74,14 +54,14 @@ def tile_visionattention_pa_s_kernel(tc, x, Wq, bq, k, out):
         wq_rows = Wq.rearrange("(a r e) c -> r a e c", r=P, e=PAIR)
         x_sb = keep.tile([P, CHANNELS], BF16)
         k_sb = keep.tile([P, CHANNELS], BF16)
-        nc.sync.dma_start(out=wq_tiles[:, 0, :], in_=wq_rows[:, 0, 0, :])
-        nc.sync.dma_start(
-            out=x_sb[:].rearrange("p (a en) -> p a en", a=GROUPS),
-            in_=x.rearrange("b c h w -> c (b h w)").rearrange(
-                "(a p e) n -> p a (e n)", p=P, e=PAIR
-            ),
-        )
-        for j in range(1, O_TILES):
+        for j in range(O_TILES):
+            if j == ROUND_TILES:
+                nc.sync.dma_start(
+                    out=x_sb[:].rearrange("p (a en) -> p a en", a=GROUPS),
+                    in_=x.rearrange("b c h w -> c (b h w)").rearrange(
+                        "(a p e) n -> p a (e n)", p=P, e=PAIR
+                    ),
+                )
             nc.sync.dma_start(out=wq_tiles[:, j, :], in_=wq_rows[:, j // PAIR, j % PAIR, :])
         nc.sync.dma_start(out=k_sb[:], in_=k.rearrange("b m c -> (b m) c"))
         wq_words = wq_sb[:].bitcast(F32).rearrange("p (j w) -> p j w", j=O_TILES)

from contextlib import ExitStack

import concourse.mybir as mybir
from concourse.masks import make_identity

F32 = mybir.dt.float32
BF16 = mybir.dt.bfloat16
U32 = mybir.dt.uint32
U8 = mybir.dt.uint8
FP8X4 = mybir.dt.float8_e4m3fn_x4
ACT = mybir.ActivationFunctionType
ALU = mybir.AluOpType
AXIS = mybir.AxisListType

P = 128
TOKENS = 128
CHANNELS = 1024
PACK = 4
K_PASS = P * PACK
PASSES = CHANNELS // K_PASS
PAIR = 2
HALVES = PACK // PAIR
GROUPS = PASSES * HALVES
O_TILES = CHANNELS // P
TILES_PER_PASS = O_TILES // PASSES
ROUND_TILES = 4
ROUNDS = O_TILES // ROUND_TILES
ROUNDS_PER_PASS = TILES_PER_PASS // ROUND_TILES

FLOPS = 2 * TOKENS * CHANNELS * CHANNELS + 2 * TOKENS * TOKENS * CHANNELS


def tile_visionattention_pa_s_kernel(tc, x, Wq, bq, k, out):
    nc = tc.nc
    with ExitStack() as ctx:
        ctx.enter_context(tc.manual_schedule())
        keep = ctx.enter_context(tc.tile_pool(name="keep", bufs=1))
        per_tile = ctx.enter_context(tc.tile_pool(name="per_tile", bufs=O_TILES))
        per_pass = ctx.enter_context(tc.tile_pool(name="per_pass", bufs=PASSES))
        psum_t = ctx.enter_context(tc.psum_pool(name="psum_t", bufs=4))
        psum_q = ctx.enter_context(tc.psum_pool(name="psum_q", bufs=PASSES))
        psum_one = ctx.enter_context(tc.psum_pool(name="psum_one", bufs=1))

        bq_rows = keep.tile([P, PAIR * P], BF16)
        nc.vector.memset(bq_rows[:], 0.0)
        zero_col = keep.tile([P, 1], F32)
        nc.vector.memset(zero_col[:], 0.0)
        nc.scalar.dma_start(
            out=bq_rows[0:GROUPS, :], in_=bq.rearrange("(a w) -> a w", a=GROUPS)
        )

        wq_sb = keep.tile([P, O_TILES * CHANNELS], BF16)
        wq_tiles = wq_sb[:].rearrange("p (j c) -> p j c", j=O_TILES)
        wq_rows = Wq.rearrange("(a r e) c -> r a e c", r=P, e=PAIR)
        x_sb = keep.tile([P, CHANNELS], BF16)
        k_sb = keep.tile([P, CHANNELS], BF16)
        for j in range(O_TILES):
            if j == ROUND_TILES:
                nc.sync.dma_start(
                    out=x_sb[:].rearrange("p (a en) -> p a en", a=GROUPS),
                    in_=x.rearrange("b c h w -> c (b h w)").rearrange(
                        "(a p e) n -> p a (e n)", p=P, e=PAIR
                    ),
                )
            nc.sync.dma_start(out=wq_tiles[:, j, :], in_=wq_rows[:, j // PAIR, j % PAIR, :])
        nc.sync.dma_start(out=k_sb[:], in_=k.rearrange("b m c -> (b m) c"))
        wq_words = wq_sb[:].bitcast(F32).rearrange("p (j w) -> p j w", j=O_TILES)
        k_words = k_sb[:].bitcast(F32)

        ident = keep.tile([P, P], F32)
        make_identity(nc, ident[:])

        warm = keep.tile([P, 1], F32)
        nc.scalar.activation(out=warm[:], in_=zero_col[:], func=ACT.Exp)

        x_grouped = keep.tile([P, PASSES * TOKENS * PACK], BF16, align_bytes=64)
        nc.vector.tensor_copy(
            out=x_grouped[:].rearrange("p (g n t) -> p g n t", g=PASSES, t=PACK),
            in_=x_sb[:].rearrange("p (g t n) -> p g n t", g=PASSES, t=PACK),
        )
        x_codes = keep.tile([P, PASSES * TOKENS], U32, align_bytes=64)
        x_scales = keep.tile([P, PASSES * TOKENS], U8, align_bytes=64)
        nc.vector.quantize_mx(out=x_codes[:].bitcast(FP8X4), scales=x_scales[:], in_=x_grouped[:])

        def transpose_rows(words):
            bank = psum_t.tile([P, PASSES, HALVES, P], F32)
            for g in range(PASSES):
                for u in range(HALVES):
                    first = (g * HALVES + u) * P
                    nc.tensor.transpose(bank[:, g, u, :], words[:, first : first + P], ident[:])
            return bank

        def empty_bank(bank):
            grouped = per_tile.tile([P, PASSES * P * PACK], BF16, align_bytes=64, bufs=O_TILES + 1)
            nc.scalar.copy(
                out=grouped[:].bitcast(F32).rearrange("p (g r u) -> p g r u", g=PASSES, u=HALVES),
                in_=bank[:].rearrange("p g u r -> p g r u"),
            )
            return grouped

        def quantise_rows(grouped):
            codes = per_tile.tile([P, PASSES * P], U32, align_bytes=64, bufs=O_TILES + 1)
            scales = per_tile.tile([P, PASSES * P], U8, align_bytes=64, bufs=O_TILES + 1)
            nc.vector.quantize_mx(out=codes[:].bitcast(FP8X4), scales=scales[:], in_=grouped[:])
            return codes, scales

        qT = []
        for g in range(PASSES):
            q_bank = psum_q.tile([P, TILES_PER_PASS, TOKENS], F32)
            qT.append(q_bank)

        def project_tile(j, codes, scales):
            for g in range(PASSES):
                cols = slice(g * P, (g + 1) * P)
                nc.tensor.matmul_mx(
                    out=qT[j // TILES_PER_PASS][:, j % TILES_PER_PASS, :],
                    lhsT=codes[:, cols].bitcast(FP8X4),
                    lhsT_scale=scales[:, cols],
                    rhs=x_codes[:, cols].bitcast(FP8X4),
                    rhs_scale=x_scales[:, cols],
                    start=(g == 0),
                    stop=(g == PASSES - 1),
                )

        bias = keep.tile([P, O_TILES], F32)

        def finish_q_pass(g):
            grouped = per_pass.tile([P, TOKENS * PACK], BF16, align_bytes=64)
            nc.vector.scalar_tensor_tensor(
                out=grouped[:].rearrange("p (n t) -> p n t", t=PACK),
                in0=qT[g][:].rearrange("p t n -> p n t"),
                scalar=1.0 / 32.0,
                in1=bias[:, g * PACK : (g + 1) * PACK].unsqueeze(1).to_broadcast([P, TOKENS, PACK]),
                op0=ALU.mult,
                op1=ALU.add,
            )
            codes = per_pass.tile([P, TOKENS], U32, align_bytes=64)
            scales = per_pass.tile([P, TOKENS], U8, align_bytes=64)
            nc.vector.quantize_mx(out=codes[:].bitcast(FP8X4), scales=scales[:], in_=grouped[:])
            return codes, scales

        def tiles_of_round(a):
            if 0 <= a < ROUNDS:
                return range(a * ROUND_TILES, (a + 1) * ROUND_TILES)
            return range(0)

        banks = {}
        grouped_rows = {}
        quantised = {}
        q_quantised = {}
        for a in range(ROUNDS + 2):
            for j in tiles_of_round(a):
                banks[j] = transpose_rows(wq_words[:, j, :])
            if a == 0:
                bqT = psum_one.tile([P, P], F32, tag="small")
                nc.tensor.transpose(bqT[:], bq_rows[:].bitcast(F32), ident[:])
                nc.vector.tensor_scalar(
                    out=bias[:],
                    in0=bqT[:, 0:GROUPS].bitcast(BF16),
                    scalar1=1.0 / 32.0,
                    scalar2=None,
                    op0=ALU.mult,
                )
            if a == ROUNDS:
                banks["k"] = transpose_rows(k_words)
            for j in tiles_of_round(a - 1):
                quantised[j] = quantise_rows(grouped_rows[j])
            if a == ROUNDS + 1:
                quantised["k"] = quantise_rows(grouped_rows["k"])
            if a >= 2 and (a - 1) % ROUNDS_PER_PASS == 0:
                g = (a - 1) // ROUNDS_PER_PASS - 1
                q_quantised[g] = finish_q_pass(g)
            for j in tiles_of_round(a):
                grouped_rows[j] = empty_bank(banks[j])
            if a == ROUNDS:
                grouped_rows["k"] = empty_bank(banks["k"])
            for j in tiles_of_round(a - 1):
                project_tile(j, quantised[j][0], quantised[j][1])

        scores = psum_one.tile([P, TOKENS], F32, tag="small")
        for g in range(PASSES):
            cols = slice(g * TOKENS, (g + 1) * TOKENS)
            nc.tensor.matmul_mx(
                out=scores[:],
                lhsT=q_quantised[g][0][:].bitcast(FP8X4),
                lhsT_scale=q_quantised[g][1][:],
                rhs=quantised["k"][0][:, cols].bitcast(FP8X4),
                rhs_scale=quantised["k"][1][:, cols],
                start=(g == 0),
                stop=(g == PASSES - 1),
            )

        neg_max = keep.tile([P, 1], F32)
        nc.vector.tensor_reduce(out=neg_max[:], in_=scores[:], axis=AXIS.X, op=ALU.max, negate=True)
        expo = keep.tile([P, TOKENS], F32)
        row_sum = keep.tile([P, 1], F32)
        nc.scalar.activation(
            out=expo[:], in_=scores[:], func=ACT.Exp, bias=neg_max[:], scale=1.0, accum_out=row_sum[:]
        )
        inv_sum = keep.tile([P, 1], F32)
        nc.vector.reciprocal(out=inv_sum[:], in_=row_sum[:])
        prob = keep.tile([P, TOKENS], F32)
        nc.vector.tensor_scalar(
            out=prob[:], in0=expo[:], scalar1=inv_sum[:, 0:1], scalar2=None, op0=ALU.mult
        )
        nc.sync.dma_start(out=out.rearrange("b n m -> (b n) m"), in_=prob[:])
